import numpy as np
import ml_dtypes


def mxq(x, axis, fmt="e4m3"):
    dtype, down = {"e4m3": (ml_dtypes.float8_e4m3fn, 7), "e5m2": (ml_dtypes.float8_e5m2, 14)}[fmt]
    v = np.moveaxis(np.asarray(x, np.float32).astype(ml_dtypes.bfloat16).astype(np.float64), axis, -1)
    blocks = v.reshape(v.shape[:-1] + (-1, 32))
    amax = np.abs(blocks).max(-1, keepdims=True)
    byte = np.maximum(np.where(amax > 0, np.frexp(amax)[1] - 1 + 127, 0) - down, 1)
    scale = np.exp2(byte - 127.0)
    codes = (blocks / scale).astype(np.float32).astype(dtype).astype(np.float64)
    return np.moveaxis((codes * scale).reshape(v.shape), -1, axis)


WIDE = False


def mx_kscale(k):
    if not WIDE:
        return np.ones(k)
    levels = np.array([10, -10, 5, -5, 0])
    if k % 512:
        return np.exp2(np.random.permutation(np.resize(levels, k // 32))).repeat(32)
    a = np.empty((k // 512, 16))
    for p in range(k // 512):
        a[p, :8] = np.random.permutation(np.resize(levels, 8))
        for g in range(8):
            far = levels[np.abs(levels - a[p, g]) >= 10]
            a[p, g + 8] = far[np.random.randint(len(far))]
    return np.exp2(a.ravel()).repeat(32)


BF16 = ml_dtypes.bfloat16


def bf(x):
    return np.asarray(x, np.float32).astype(BF16)


def f64(x):
    return np.asarray(x).astype(np.float64)


E2M1 = np.array([0.0, 0.5, 1.0, 1.5, 2.0, 3.0, 4.0, 6.0, -0.0, -0.5, -1.0, -1.5, -2.0, -3.0, -4.0, -6.0])


def pack_weight(w, fmt):
    k, n = w.shape
    w = f64(bf(w)).reshape(k // 32, 32, n)
    amax = np.abs(w).max(1)
    if fmt == "e4m3":
        byte = np.frexp(amax)[1] - 1 + 127 - 7
    else:
        mant, ex = np.frexp(amax / 6.0)
        byte = np.where(mant > 0.5, ex, ex - 1) + 127
    byte = np.clip(np.where(amax > 0, byte, 1), 1, 254)
    scaled = (w * np.exp2(127.0 - byte)[:, None, :]).reshape(k, n).astype(np.float32)
    by_word = np.ascontiguousarray(scaled.reshape(k // 512, 128, 4, n).transpose(0, 1, 3, 2))
    if fmt == "e4m3":
        words = by_word.astype(ml_dtypes.float8_e4m3fn).view(np.uint8)
    else:
        c = by_word.astype(ml_dtypes.float4_e2m1fn).view(np.uint8) & 0xF
        words = c[..., 0::2] | (c[..., 1::2] << 4)
    return np.ascontiguousarray(words), np.ascontiguousarray(byte.astype(np.uint8).reshape(k // 512, 16, n))


def unpack_weight(words, scales, fmt):
    g, p, n, _ = words.shape
    if fmt == "e4m3":
        vals = np.ascontiguousarray(words).view(ml_dtypes.float8_e4m3fn).astype(np.float64)
    else:
        nib = np.empty((g, p, n, 4), np.uint8)
        nib[..., 0::2] = words & 0xF
        nib[..., 1::2] = words >> 4
        vals = E2M1[nib]
    vals = vals * np.repeat(np.exp2(scales.astype(np.float64) - 127.0), 8, axis=1)[..., None]
    return vals.transpose(0, 1, 3, 2).reshape(g * 512, n)
def pack4(w):
    words, scales = pack_weight(w, "e2m1")
    return words.reshape(words.shape[0], 128, -1), scales


def unpack4(words, scales):
    return unpack_weight(words.reshape(words.shape[0], 128, -1, 2), scales, "e2m1")


B, M, H_ENC, N, H_DEC = 8192, 512, 512, 128, 128
SNR = 25.0
NOISE_STD = float(np.sqrt(1.0 / (2.0 * 10.0 ** (SNR / 10.0))))


def draw0():
    s = mx_kscale(M)
    t = mx_kscale(H_ENC)
    theta = np.random.uniform(0.3, 1.2)
    x = bf(np.random.standard_normal((B, M)) * s)
    noise = bf(np.random.standard_normal((B, N)) * NOISE_STD)
    h = bf(np.array([np.cos(theta), np.sin(theta)]))
    W1 = np.random.standard_normal((H_ENC, M)) / np.sqrt(M) / s[None, :] * t[:, None]
    W1_words, W1_scales = pack4(W1.T)
    b1 = bf(np.random.standard_normal(H_ENC) * 0.3 * t)
    W2 = np.random.standard_normal((N, H_ENC)) / np.sqrt(H_ENC) / t[None, :]
    W2_words, W2_scales = pack4(W2.T)
    b2 = bf(np.random.standard_normal(N) * 0.3)
    return {"x": x,
            "noise": noise,
            "h": h,
            "W1_words": W1_words,
            "W1_scales": W1_scales,
            "b1": b1,
            "W2_words": W2_words,
            "W2_scales": W2_scales,
            "b2": b2}


def core(x, noise, h, W1_words, W1_scales, b1, W2_words, W2_scales, b2):
    h = f64(h)
    a = np.maximum((mxq(f64(x), 1, "e4m3") @ unpack4(W1_words, W1_scales)) + f64(b1), 0.0)
    z = (mxq(a, 1, "e4m3") @ unpack4(W2_words, W2_scales)) + f64(b2)
    scale = np.sqrt(N * 0.5)
    z = scale * z / np.linalg.norm(z, axis=1, keepdims=True)
    zc = z.reshape(B, N // 2, 2)
    yr = zc[..., 0] * h[0] - zc[..., 1] * h[1]
    yi = zc[..., 0] * h[1] + zc[..., 1] * h[0]
    y = np.stack([yr, yi], axis=-1).reshape(B, N)
    return y + f64(noise)


def e4m3fn_bytes(y):
    return np.clip(np.asarray(y, np.float64), -448.0, 448.0).astype(np.float32).astype(ml_dtypes.float8_e4m3fn).view(np.uint8)


def e4m3fn_values(b):
    return np.asarray(b, np.uint8).view(ml_dtypes.float8_e4m3fn).astype(np.float64)


def setup_inputs():
    d = draw0()
    x0 = np.asarray(d['x']).astype(np.float64)
    s = (np.max(np.abs(x0), axis=(0,), keepdims=True) / 448.0).astype(np.float32)
    out = {}
    for k, v in d.items():
        if k == 'x':
            out['x_bytes'] = e4m3fn_bytes(x0 / s.astype(np.float64))
            out['x_scale'] = s
        else:
            out[k] = v
    return out


def reference(x_bytes, x_scale, noise, h, W1_words, W1_scales, b1, W2_words, W2_scales, b2):
    return core(e4m3fn_values(x_bytes) * x_scale.astype(np.float64), noise, h, W1_words, W1_scales, b1, W2_words, W2_scales, b2)

@@ -1,0 +1,311 @@
+from contextlib import ExitStack
+
+import concourse.mybir as mybir
+from concourse.masks import make_identity
+
+F32 = mybir.dt.float32
+BF16 = mybir.dt.bfloat16
+I32 = mybir.dt.int32
+U32 = mybir.dt.uint32
+U8 = mybir.dt.uint8
+E4M3 = mybir.dt.float8_e4m3fn
+E4M3X4 = mybir.dt.float8_e4m3fn_x4
+E2M1X4 = mybir.dt.float4_e2m1fn_x4
+ACT = mybir.ActivationFunctionType
+ALU = mybir.AluOpType
+
+P = 128
+TOKENS = 8192
+K1 = 512
+HID = 512
+CH = 128
+PACK = 4
+
+CHUNK = 256
+SLOTS = CHUNK // P
+GROUPS = [256, 256, 512] + [1024] * 7
+
+FLOPS = 2 * TOKENS * HID * (K1 + CH)
+
+
+def tile_channel_net_pa_w4_kernel(
+    tc, x_bytes, x_scale, noise, h, W1_words, W1_scales, b1, W2_words, W2_scales, b2, out
+):
+    nc = tc.nc
+    with ExitStack() as ctx:
+        const = ctx.enter_context(tc.tile_pool(name="const", bufs=1))
+        data = ctx.enter_context(tc.tile_pool(name="data", bufs=1))
+        work = ctx.enter_context(tc.tile_pool(name="work", bufs=3))
+        psum = ctx.enter_context(tc.psum_pool(name="psum", bufs=1))
+
+        x_sb, noise_sb, chunk_home = [], [], []
+        base = 0
+        loads = []
+        for g, size in enumerate(GROUPS):
+            slots = size // P
+            xt = data.tile([P, slots * K1], U8, name="x_%d" % g)
+            nt = data.tile([P, slots, CH], BF16, name="noise_%d" % g)
+            x_sb.append(xt)
+            noise_sb.append(nt)
+            loads.append((xt, nt, base, size, slots))
+            for c in range(size // CHUNK):
+                chunk_home.append((g, c * SLOTS))
+            base += size
+
+        def load_x(g):
+            xt, nt, b, size, slots = loads[g]
+            nc.sync.dma_start(out=xt[:], in_=x_bytes[b : b + size, :].rearrange("(p j) k -> p (j k)", j=slots))
+
+        def load_noise(g):
+            xt, nt, b, size, slots = loads[g]
+            nc.sync.dma_start(out=nt[:], in_=noise[b : b + size, :].rearrange("(p j) n -> p j n", j=slots))
+
+        sc = const.tile([P, PACK], F32, name="sc")
+        w1_raw = const.tile([P, HID * 2], U8, name="w1_raw")
+        w1 = const.tile([P, HID * 2], U8, name="w1", align_bytes=64)
+        s_raw = const.tile([P, HID + CH], U8, name="s_raw", align_bytes=64)
+        s1 = const.tile([P, HID], U8, name="s1", align_bytes=64)
+        w2 = const.tile([P, CH * 2], U8, name="w2", align_bytes=64)
+        b1_raw = const.tile([P, PACK], BF16, name="b1_raw")
+        b1f = const.tile([P, PACK], F32, name="b1f")
+        b2_raw = const.tile([P, 1], BF16, name="b2_raw")
+        b2f = const.tile([P, 1], F32, name="b2f")
+        h_raw = const.tile([P, 2], BF16, name="h_raw")
+        hf = const.tile([P, 2], F32, name="hf")
+        ident = const.tile([P, P], F32, name="ident")
+        rot = const.tile([P, P], F32, name="rot")
+        rot_d = const.tile([P, P], F32, name="rot_d")
+        nh1 = const.tile([P, 1], F32, name="nh1")
+        hsq = const.tile([P, 2], F32, name="hsq")
+        hs = const.tile([P, 1], F32, name="hs")
+        flag = const.tile([P, 1], F32, name="flag")
+        den = const.tile([P, 1], F32, name="den")
+        inv = const.tile([P, 1], F32, name="inv")
+        warm = const.tile([P, 1], F32, name="warm")
+
+        nc.vector.memset(s_raw[:].bitcast(I32), 0)
+        nc.vector.memset(warm[:], 1.0)
+        make_identity(nc, ident[:])
+        nc.scalar.activation(out=warm[:], in_=warm[:], func=ACT.Abs_reciprocal_sqrt)
+
+        load_x(0)
+        nc.sync.dma_start(out=sc[:], in_=x_scale.rearrange("o (p t) -> p (o t)", t=PACK))
+        nc.sync.dma_start(out=w1_raw[:], in_=W1_words[0])
+        for q in range(4):
+            nc.sync.dma_start(
+                out=s_raw[32 * q : 32 * q + 4, 0:HID].bitcast(I32),
+                in_=W1_scales[0, 4 * q : 4 * q + 4, :].bitcast(I32),
+            )
+        load_x(1)
+        nc.sync.dma_start(out=b1_raw[:], in_=b1.rearrange("(p t) -> p t", t=PACK))
+        load_x(2)
+        nc.sync.dma_start(out=w2[:], in_=W2_words[0])
+        for q in range(4):
+            nc.sync.dma_start(
+                out=s_raw[32 * q : 32 * q + 4, HID : HID + CH].bitcast(I32),
+                in_=W2_scales[0, 4 * q : 4 * q + 4, :].bitcast(I32),
+            )
+        nc.sync.dma_start(out=b2_raw[:], in_=b2.rearrange("(p o) -> p o", o=1))
+        nc.sync.dma_start(out=h_raw[:], in_=h.partition_broadcast(P))
+        load_noise(0)
+        load_noise(1)
+        load_noise(2)
+        for g in range(3, len(GROUPS)):
+            load_x(g)
+            load_noise(g)
+
+        nc.vector.tensor_copy(
+            out=w1[:].rearrange("p (t m b) -> p m t b", t=PACK, b=2),
+            in_=w1_raw[:].rearrange("p (m t b) -> p m t b", t=PACK, b=2),
+        )
+        nc.vector.tensor_copy(
+            out=s1[:].rearrange("p (t m) -> p m t", t=PACK),
+            in_=s_raw[:, 0:HID].rearrange("p (m t) -> p m t", t=PACK),
+        )
+        nc.vector.tensor_copy(out=b1f[:], in_=b1_raw[:])
+
+        def late_constants():
+            nc.vector.tensor_copy(out=b2f[:], in_=b2_raw[:])
+            nc.vector.tensor_copy(out=hf[:], in_=h_raw[:])
+            nc.vector.tensor_scalar(out=nh1[:], in0=hf[:, 1:2], scalar1=-1.0, scalar2=None, op0=ALU.mult)
+            nc.vector.tensor_tensor(out=hsq[:], in0=hf[:], in1=hf[:], op=ALU.mult)
+            nc.vector.tensor_scalar(out=rot_d[:], in0=ident[:], scalar1=hf[:, 0:1], scalar2=None, op0=ALU.mult)
+            nc.vector.tensor_tensor(out=hs[:], in0=hsq[:, 0:1], in1=hsq[:, 1:2], op=ALU.add)
+            nc.vector.scalar_tensor_tensor(
+                out=rot[:, 0::2], in0=ident[:, 1::2], scalar=nh1[:], in1=rot_d[:, 0::2], op0=ALU.mult, op1=ALU.add
+            )
+            nc.vector.tensor_scalar(out=flag[:], in0=hs[:], scalar1=0.0, scalar2=None, op0=ALU.is_equal)
+            nc.vector.scalar_tensor_tensor(
+                out=rot[:, 1::2], in0=ident[:, 0::2], scalar=hf[:, 1:2], in1=rot_d[:, 1::2], op0=ALU.mult, op1=ALU.add
+            )
+            nc.vector.scalar_tensor_tensor(
+                out=den[:], in0=hs[:], scalar=64.0, in1=flag[:], op0=ALU.mult, op1=ALU.add
+            )
+            nc.vector.reciprocal(out=inv[:], in_=den[:])
+
+        st = {}
+
+        def widen(c):
+            g, j = chunk_home[c]
+            xw = work.tile([P, SLOTS * K1], BF16, name="xw")
+            nc.scalar.copy(out=xw[:], in_=x_sb[g][:, j * K1 : (j + SLOTS) * K1].bitcast(E4M3))
+            st["xw", c] = xw
+
+        def transposes(c):
+            words = st.pop(("xw", c))[:].bitcast(F32)
+            xt = psum.tile([P, 2, CHUNK], F32, name="xt", bufs=2)
+            for j in range(SLOTS):
+                for u in range(2):
+                    nc.tensor.transpose(
+                        xt[:, u, j * P : (j + 1) * P],
+                        words[:, 256 * j + u : 256 * (j + 1) : 2],
+                        ident[:],
+                    )
+            st["xt", c] = xt
+
+        def scale_x(c):
+            xt = st.pop(("xt", c))
+            xs = work.tile([P, CHUNK, 2, 2], BF16, name="xs", align_bytes=64)
+            nc.vector.tensor_tensor(
+                out=xs[:],
+                in0=xt[:].bitcast(BF16).rearrange("p u (n e) -> p n u e", e=2),
+                in1=sc[:].rearrange("p (u e) -> p u e", e=2).unsqueeze(1).to_broadcast([P, CHUNK, 2, 2]),
+                op=ALU.mult,
+            )
+            st["xs", c] = xs
+
+        def quant_x(c):
+            xs = st.pop(("xs", c))
+            xq = work.tile([P, CHUNK], U32, name="xq", align_bytes=64)
+            xqs = work.tile([P, CHUNK], U8, name="xqs", align_bytes=64)
+            nc.vector.quantize_mx(
+                out=xq[:].bitcast(E4M3X4), scales=xqs[:], in_=xs[:].rearrange("p n u e -> p (n u e)")
+            )
+            st["xq", c] = (xq, xqs)
+
+        def first_matmul(c):
+            xq, xqs = st.pop(("xq", c))
+            banks = []
+            for b in range(2):
+                bank = psum.tile([P, 2, CHUNK], F32, name="hid", bufs=4)
+                for i in range(2):
+                    t = 2 * b + i
+                    nc.tensor.matmul_mx(
+                        out=bank[:, i, :],
+                        lhsT=w1[:, 256 * t : 256 * (t + 1)].bitcast(E2M1X4),
+                        lhsT_scale=s1[:, P * t : P * (t + 1)],
+                        rhs=xq[:].bitcast(E4M3X4),
+                        rhs_scale=xqs[:],
+                        start=True,
+                        stop=True,
+                    )
+                banks.append(bank)
+            st["hid", c] = banks
+
+        def relu(c):
+            banks = st.pop(("hid", c))
+            planes = work.tile([P, PACK, CHUNK], BF16, name="planes")
+            for t in range(PACK):
+                nc.scalar.activation(
+                    out=planes[:, t, :], in_=banks[t // 2][:, t % 2, :], func=ACT.Relu, bias=b1f[:, t : t + 1]
+                )
+            st["planes", c] = planes
+
+        def interleave(c):
+            planes = st.pop(("planes", c))
+            ai = work.tile([P, CHUNK, PACK], BF16, name="ai", align_bytes=64)
+            nc.gpsimd.tensor_scalar(
+                out=ai[:], in0=planes[:].rearrange("p t n -> p n t"), scalar1=1.0, scalar2=0.0, op0=ALU.mult, op1=ALU.add
+            )
+            st["ai", c] = ai
+
+        def quant_a(c):
+            ai = st.pop(("ai", c))
+            aq = work.tile([P, CHUNK], U32, name="aq", align_bytes=64)
+            aqs = work.tile([P, CHUNK], U8, name="aqs", align_bytes=64)
+            nc.vector.quantize_mx(out=aq[:].bitcast(E4M3X4), scales=aqs[:], in_=ai[:].rearrange("p n t -> p (n t)"))
+            st["aq", c] = (aq, aqs)
+
+        def second_matmul(c):
+            aq, aqs = st.pop(("aq", c))
+            z = psum.tile([P, CHUNK], F32, name="z", bufs=1)
+            nc.tensor.matmul_mx(
+                out=z[:],
+                lhsT=w2[:].bitcast(E2M1X4),
+                lhsT_scale=s_raw[:, HID : HID + CH],
+                rhs=aq[:].bitcast(E4M3X4),
+                rhs_scale=aqs[:],
+                start=True,
+                stop=True,
+            )
+            st["z", c] = z
+
+        def bias_z(c):
+            z = st.pop(("z", c))
+            zb = work.tile([P, CHUNK], F32, name="zb")
+            nc.scalar.activation(out=zb[:], in_=z[:], func=ACT.Identity, bias=b2f[:])
+            st["zb", c] = zb
+
+        def rotate(c):
+            zb = st.pop(("zb", c))
+            r = psum.tile([P, SLOTS, CH], F32, name="r", bufs=1)
+            for j in range(SLOTS):
+                nc.tensor.matmul(
+                    out=r[:, j, :], lhsT=zb[:, j * P : (j + 1) * P], rhs=rot[:], start=True, stop=True
+                )
+            st["r", c] = r
+
+        def norms(c):
+            r = st["r", c]
+            ss = work.tile([P, SLOTS], F32, name="ss")
+            gain = work.tile([P, SLOTS], F32, name="gain")
+            for j in range(SLOTS):
+                junk = work.tile([P, CH], BF16, name="junk")
+                nc.scalar.activation(out=junk[:], in_=r[:, j, :], func=ACT.Square, accum_out=ss[:, j : j + 1])
+            nc.scalar.activation(
+                out=gain[:], in_=ss[:], func=ACT.Abs_reciprocal_sqrt, scale=inv[:], bias=flag[:]
+            )
+            st["gain", c] = gain
+
+        def finish(c):
+            g, j0 = chunk_home[c]
+            r = st.pop(("r", c))
+            gain = st.pop(("gain", c))
+            y = work.tile([P, SLOTS, CH], F32, name="y")
+            for j in range(SLOTS):
+                nc.vector.scalar_tensor_tensor(
+                    out=y[:, j, :],
+                    in0=r[:, j, :],
+                    scalar=gain[:, j : j + 1],
+                    in1=noise_sb[g][:, j0 + j, :],
+                    op0=ALU.mult,
+                    op1=ALU.add,
+                )
+            b, size, slots = loads[g][2:]
+            dst = out[b : b + size, :].rearrange("(p j) n -> p j n", j=slots)
+            nc.sync.dma_start(out=dst[:, j0 : j0 + SLOTS, :], in_=y[:])
+
+        n = TOKENS // CHUNK
+        order = [
+            (finish, 4),
+            (second_matmul, 2),
+            (relu, 0),
+            (rotate, 3),
+            (bias_z, 2),
+            (norms, 3),
+            (transposes, -2),
+            (scale_x, -1),
+            (widen, -3),
+            (quant_x, -1),
+            (interleave, 1),
+            (quant_a, 1),
+            (first_matmul, -1),
+        ]
+        with tc.manual_schedule():
+            for s in range(-3, n + 5):
+                if s == 0:
+                    late_constants()
+                for stage, lag in order:
+                    c = s - lag
+                    if 0 <= c < n:
+                        stage(c)

@@ -21,9 +21,9 @@ HID = 512
 CH = 128
 PACK = 4
 
-CHUNK = 256
-SLOTS = CHUNK // P
-GROUPS = [256, 256, 512] + [1024] * 7
+CHUNKS = [256, 256] + [512] * 14 + [256, 256]
+GROUPS = [[256], [256], [512]] + [[512, 512]] * 6 + [[512, 256, 256]]
+BANK = 256
 
 FLOPS = 2 * TOKENS * HID * (K1 + CH)
 
@@ -41,15 +41,18 @@ def tile_channel_net_pa_w4_kernel(
         x_sb, noise_sb, chunk_home = [], [], []
         base = 0
         loads = []
-        for g, size in enumerate(GROUPS):
+        for g, parts in enumerate(GROUPS):
+            size = sum(parts)
             slots = size // P
             xt = data.tile([P, slots * K1], U8, name="x_%d" % g)
             nt = data.tile([P, slots, CH], BF16, name="noise_%d" % g)
             x_sb.append(xt)
             noise_sb.append(nt)
             loads.append((xt, nt, base, size, slots))
-            for c in range(size // CHUNK):
-                chunk_home.append((g, c * SLOTS))
+            j = 0
+            for part in parts:
+                chunk_home.append((g, j, part // P))
+                j += part // P
             base += size
 
         def load_x(g):
@@ -146,38 +149,51 @@ def tile_channel_net_pa_w4_kernel(
         st = {}
 
         def widen(c):
-            g, j = chunk_home[c]
-            xw = work.tile([P, SLOTS * K1], BF16, name="xw")
-            nc.scalar.copy(out=xw[:], in_=x_sb[g][:, j * K1 : (j + SLOTS) * K1].bitcast(E4M3))
+            g, j, slots = chunk_home[c]
+            half = slots // 2
+            xw = work.tile([P, slots * K1], BF16, name="xw")
+            nc.scalar.copy(
+                out=xw[:, half * K1 :], in_=x_sb[g][:, (j + half) * K1 : (j + slots) * K1].bitcast(E4M3)
+            )
             st["xw", c] = xw
+
+        def widen_v(c):
+            g, j, slots = chunk_home[c]
+            half = slots // 2
+            xw = st["xw", c]
+            nc.vector.tensor_copy(out=xw[:, : half * K1], in_=x_sb[g][:, j * K1 : (j + half) * K1].bitcast(E4M3))
 
         def transposes(c):
             words = st.pop(("xw", c))[:].bitcast(F32)
-            xt = psum.tile([P, 2, CHUNK], F32, name="xt", bufs=2)
-            for j in range(SLOTS):
-                for u in range(2):
-                    nc.tensor.transpose(
-                        xt[:, u, j * P : (j + 1) * P],
-                        words[:, 256 * j + u : 256 * (j + 1) : 2],
-                        ident[:],
-                    )
-            st["xt", c] = xt
+            banks = []
+            for j0 in range(0, chunk_home[c][2], 2):
+                xt = psum.tile([P, 2, BANK], F32, name="xt", bufs=2)
+                for j in range(2):
+                    for u in range(2):
+                        nc.tensor.transpose(
+                            xt[:, u, j * P : (j + 1) * P],
+                            words[:, 256 * (j0 + j) + u : 256 * (j0 + j + 1) : 2],
+                            ident[:],
+                        )
+                banks.append(xt)
+            st["xt", c] = banks
 
         def scale_x(c):
-            xt = st.pop(("xt", c))
-            xs = work.tile([P, CHUNK, 2, 2], BF16, name="xs", align_bytes=64)
-            nc.vector.tensor_tensor(
-                out=xs[:],
-                in0=xt[:].bitcast(BF16).rearrange("p u (n e) -> p n u e", e=2),
-                in1=sc[:].rearrange("p (u e) -> p u e", e=2).unsqueeze(1).to_broadcast([P, CHUNK, 2, 2]),
-                op=ALU.mult,
-            )
+            banks = st.pop(("xt", c))
+            xs = work.tile([P, CHUNKS[c], 2, 2], BF16, name="xs", align_bytes=64)
+            for i, xt in enumerate(banks):
+                nc.vector.tensor_tensor(
+                    out=xs[:, i * BANK : (i + 1) * BANK],
+                    in0=xt[:].bitcast(BF16).rearrange("p u (n e) -> p n u e", e=2),
+                    in1=sc[:].rearrange("p (u e) -> p u e", e=2).unsqueeze(1).to_broadcast([P, BANK, 2, 2]),
+                    op=ALU.mult,
+                )
             st["xs", c] = xs
 
         def quant_x(c):
             xs = st.pop(("xs", c))
-            xq = work.tile([P, CHUNK], U32, name="xq", align_bytes=64)
-            xqs = work.tile([P, CHUNK], U8, name="xqs", align_bytes=64)
+            xq = work.tile([P, CHUNKS[c]], U32, name="xq", align_bytes=64)
+            xqs = work.tile([P, CHUNKS[c]], U8, name="xqs", align_bytes=64)
             nc.vector.quantize_mx(
                 out=xq[:].bitcast(E4M3X4), scales=xqs[:], in_=xs[:].rearrange("p n u e -> p (n u e)")
             )
@@ -186,10 +202,11 @@ def tile_channel_net_pa_w4_kernel(
         def first_matmul(c):
             xq, xqs = st.pop(("xq", c))
             banks = []
-            for b in range(2):
-                bank = psum.tile([P, 2, CHUNK], F32, name="hid", bufs=4)
-                for i in range(2):
-                    t = 2 * b + i
+            per = 512 // CHUNKS[c]
+            for b in range(PACK // per):
+                bank = psum.tile([P, per, CHUNKS[c]], F32, name="hid", bufs=4)
+                for i in range(per):
+                    t = per * b + i
                     nc.tensor.matmul_mx(
                         out=bank[:, i, :],
                         lhsT=w1[:, 256 * t : 256 * (t + 1)].bitcast(E2M1X4),
@@ -204,31 +221,38 @@ def tile_channel_net_pa_w4_kernel(
 
         def relu(c):
             banks = st.pop(("hid", c))
-            planes = work.tile([P, PACK, CHUNK], BF16, name="planes")
+            per = 512 // CHUNKS[c]
+            planes = work.tile([P, PACK, CHUNKS[c]], BF16, name="planes")
             for t in range(PACK):
                 nc.scalar.activation(
-                    out=planes[:, t, :], in_=banks[t // 2][:, t % 2, :], func=ACT.Relu, bias=b1f[:, t : t + 1]
+                    out=planes[:, t, :], in_=banks[t // per][:, t % per, :], func=ACT.Relu, bias=b1f[:, t : t + 1]
                 )
             st["planes", c] = planes
 
         def interleave(c):
             planes = st.pop(("planes", c))
-            ai = work.tile([P, CHUNK, PACK], BF16, name="ai", align_bytes=64)
-            nc.gpsimd.tensor_scalar(
-                out=ai[:], in0=planes[:].rearrange("p t n -> p n t"), scalar1=1.0, scalar2=0.0, op0=ALU.mult, op1=ALU.add
-            )
+            ai = work.tile([P, CHUNKS[c], PACK], BF16, name="ai", align_bytes=64, bufs=1)
+            for n0 in range(0, CHUNKS[c], BANK):
+                nc.gpsimd.tensor_scalar(
+                    out=ai[:, n0 : n0 + BANK, :],
+                    in0=planes[:, :, n0 : n0 + BANK].rearrange("p t n -> p n t"),
+                    scalar1=1.0,
+                    scalar2=0.0,
+                    op0=ALU.mult,
+                    op1=ALU.add,
+                )
             st["ai", c] = ai
 
         def quant_a(c):
             ai = st.pop(("ai", c))
-            aq = work.tile([P, CHUNK], U32, name="aq", align_bytes=64)
-            aqs = work.tile([P, CHUNK], U8, name="aqs", align_bytes=64)
+            aq = work.tile([P, CHUNKS[c]], U32, name="aq", align_bytes=64)
+            aqs = work.tile([P, CHUNKS[c]], U8, name="aqs", align_bytes=64)
             nc.vector.quantize_mx(out=aq[:].bitcast(E4M3X4), scales=aqs[:], in_=ai[:].rearrange("p n t -> p (n t)"))
             st["aq", c] = (aq, aqs)
 
         def second_matmul(c):
             aq, aqs = st.pop(("aq", c))
-            z = psum.tile([P, CHUNK], F32, name="z", bufs=1)
+            z = psum.tile([P, CHUNKS[c]], F32, name="z", bufs=1)
             nc.tensor.matmul_mx(
                 out=z[:],
                 lhsT=w2[:].bitcast(E2M1X4),
@@ -242,14 +266,15 @@ def tile_channel_net_pa_w4_kernel(
 
         def bias_z(c):
             z = st.pop(("z", c))
-            zb = work.tile([P, CHUNK], F32, name="zb")
+            zb = work.tile([P, CHUNKS[c]], F32, name="zb")
             nc.scalar.activation(out=zb[:], in_=z[:], func=ACT.Identity, bias=b2f[:])
             st["zb", c] = zb
 
         def rotate(c):
             zb = st.pop(("zb", c))
-            r = psum.tile([P, SLOTS, CH], F32, name="r", bufs=1)
-            for j in range(SLOTS):
+            slots = chunk_home[c][2]
+            r = psum.tile([P, slots, CH], F32, name="r", bufs=1)
+            for j in range(slots):
                 nc.tensor.matmul(
                     out=r[:, j, :], lhsT=zb[:, j * P : (j + 1) * P], rhs=rot[:], start=True, stop=True
                 )
@@ -257,9 +282,10 @@ def tile_channel_net_pa_w4_kernel(
 
         def norms(c):
             r = st["r", c]
-            ss = work.tile([P, SLOTS], F32, name="ss")
-            gain = work.tile([P, SLOTS], F32, name="gain")
-            for j in range(SLOTS):
+            slots = chunk_home[c][2]
+            ss = work.tile([P, slots], F32, name="ss")
+            gain = work.tile([P, slots], F32, name="gain")
+            for j in range(slots):
                 junk = work.tile([P, CH], BF16, name="junk")
                 nc.scalar.activation(out=junk[:], in_=r[:, j, :], func=ACT.Square, accum_out=ss[:, j : j + 1])
             nc.scalar.activation(
@@ -268,11 +294,11 @@ def tile_channel_net_pa_w4_kernel(
             st["gain", c] = gain
 
         def finish(c):
-            g, j0 = chunk_home[c]
+            g, j0, n_slots = chunk_home[c]
             r = st.pop(("r", c))
             gain = st.pop(("gain", c))
-            y = work.tile([P, SLOTS, CH], F32, name="y")
-            for j in range(SLOTS):
+            y = work.tile([P, n_slots, CH], F32, name="y")
+            for j in range(n_slots):
                 nc.vector.scalar_tensor_tensor(
                     out=y[:, j, :],
                     in0=r[:, j, :],
@@ -283,9 +309,9 @@ def tile_channel_net_pa_w4_kernel(
                 )
             b, size, slots = loads[g][2:]
             dst = out[b : b + size, :].rearrange("(p j) n -> p j n", j=slots)
-            nc.sync.dma_start(out=dst[:, j0 : j0 + SLOTS, :], in_=y[:])
+            nc.sync.dma_start(out=dst[:, j0 : j0 + n_slots, :], in_=y[:])
 
-        n = TOKENS // CHUNK
+        n = len(CHUNKS)
         order = [
             (finish, 4),
             (second_matmul, 2),
@@ -296,6 +322,7 @@ def tile_channel_net_pa_w4_kernel(
             (transposes, -2),
             (scale_x, -1),
             (widen, -3),
+            (widen_v, -3),
             (quant_x, -1),
             (interleave, 1),
             (quant_a, 1),

@@ -35,7 +35,7 @@ def tile_channel_net_pa_w4_kernel(
     with ExitStack() as ctx:
         const = ctx.enter_context(tc.tile_pool(name="const", bufs=1))
         data = ctx.enter_context(tc.tile_pool(name="data", bufs=1))
-        work = ctx.enter_context(tc.tile_pool(name="work", bufs=3))
+        work = ctx.enter_context(tc.tile_pool(name="work", bufs=4))
         psum = ctx.enter_context(tc.psum_pool(name="psum", bufs=1))
 
         x_sb, noise_sb, chunk_home = [], [], []
@@ -64,6 +64,7 @@ def tile_channel_net_pa_w4_kernel(
             nc.sync.dma_start(out=nt[:], in_=noise[b : b + size, :].rearrange("(p j) n -> p j n", j=slots))
 
         sc = const.tile([P, PACK], F32, name="sc")
+        scale_row = const.tile([P, 4 * K1], F32, name="scale_row")
         w1_raw = const.tile([P, HID * 2], U8, name="w1_raw")
         w1 = const.tile([P, HID * 2], U8, name="w1", align_bytes=64)
         s_raw = const.tile([P, HID + CH], U8, name="s_raw", align_bytes=64)
@@ -91,8 +92,11 @@ def tile_channel_net_pa_w4_kernel(
         make_identity(nc, ident[:])
         nc.scalar.activation(out=warm[:], in_=warm[:], func=ACT.Abs_reciprocal_sqrt)
 
+        nc.scalar.dma_start(out=sc[:], in_=x_scale.rearrange("o (t p) -> p (o t)", t=PACK))
+        nc.scalar.dma_start(out=h_raw[:], in_=h.partition_broadcast(P))
+        nc.scalar.dma_start(out=b2_raw[:], in_=b2.rearrange("(p o) -> p o", o=1))
+        nc.scalar.dma_start(out=b1_raw[:], in_=b1.rearrange("(p t) -> p t", t=PACK))
         load_x(0)
-        nc.sync.dma_start(out=sc[:], in_=x_scale.rearrange("o (p t) -> p (o t)", t=PACK))
         nc.sync.dma_start(out=w1_raw[:], in_=W1_words[0])
         for q in range(4):
             nc.sync.dma_start(
@@ -100,7 +104,6 @@ def tile_channel_net_pa_w4_kernel(
                 in_=W1_scales[0, 4 * q : 4 * q + 4, :].bitcast(I32),
             )
         load_x(1)
-        nc.sync.dma_start(out=b1_raw[:], in_=b1.rearrange("(p t) -> p t", t=PACK))
         load_x(2)
         nc.sync.dma_start(out=w2[:], in_=W2_words[0])
         for q in range(4):
@@ -108,8 +111,6 @@ def tile_channel_net_pa_w4_kernel(
                 out=s_raw[32 * q : 32 * q + 4, HID : HID + CH].bitcast(I32),
                 in_=W2_scales[0, 4 * q : 4 * q + 4, :].bitcast(I32),
             )
-        nc.sync.dma_start(out=b2_raw[:], in_=b2.rearrange("(p o) -> p o", o=1))
-        nc.sync.dma_start(out=h_raw[:], in_=h.partition_broadcast(P))
         load_noise(0)
         load_noise(1)
         load_noise(2)
@@ -117,51 +118,56 @@ def tile_channel_net_pa_w4_kernel(
             load_x(g)
             load_noise(g)
 
-        nc.vector.tensor_copy(
-            out=w1[:].rearrange("p (t m b) -> p m t b", t=PACK, b=2),
-            in_=w1_raw[:].rearrange("p (m t b) -> p m t b", t=PACK, b=2),
-        )
-        nc.vector.tensor_copy(
-            out=s1[:].rearrange("p (t m) -> p m t", t=PACK),
-            in_=s_raw[:, 0:HID].rearrange("p (m t) -> p m t", t=PACK),
-        )
+        scale_ps = psum.tile([P, 2, BANK], F32, name="xt", bufs=2)
+        scale_flat = scale_ps[:].rearrange("p u n -> p (u n)")
+        for t in range(PACK):
+            nc.tensor.transpose(scale_flat[:, t * P : (t + 1) * P], sc[:, t : t + 1].to_broadcast([P, P]), ident[:])
+        nc.vector.tensor_copy(out=scale_row[:, 0:K1], in_=scale_flat)
+        for i in range(1, 4):
+            nc.scalar.copy(out=scale_row[:, i * K1 : (i + 1) * K1], in_=scale_flat)
+
         nc.vector.tensor_copy(out=b1f[:], in_=b1_raw[:])
 
-        def late_constants():
-            nc.vector.tensor_copy(out=b2f[:], in_=b2_raw[:])
-            nc.vector.tensor_copy(out=hf[:], in_=h_raw[:])
-            nc.vector.tensor_scalar(out=nh1[:], in0=hf[:, 1:2], scalar1=-1.0, scalar2=None, op0=ALU.mult)
-            nc.vector.tensor_tensor(out=hsq[:], in0=hf[:], in1=hf[:], op=ALU.mult)
-            nc.vector.tensor_scalar(out=rot_d[:], in0=ident[:], scalar1=hf[:, 0:1], scalar2=None, op0=ALU.mult)
-            nc.vector.tensor_tensor(out=hs[:], in0=hsq[:, 0:1], in1=hsq[:, 1:2], op=ALU.add)
-            nc.vector.scalar_tensor_tensor(
-                out=rot[:, 0::2], in0=ident[:, 1::2], scalar=nh1[:], in1=rot_d[:, 0::2], op0=ALU.mult, op1=ALU.add
+        nc.vector.tensor_copy(out=b2f[:], in_=b2_raw[:])
+        nc.vector.tensor_copy(out=hf[:], in_=h_raw[:])
+        nc.vector.tensor_scalar(out=nh1[:], in0=hf[:, 1:2], scalar1=-1.0, scalar2=None, op0=ALU.mult)
+        nc.vector.tensor_tensor(out=hsq[:], in0=hf[:], in1=hf[:], op=ALU.mult)
+        nc.vector.tensor_scalar(out=rot_d[:], in0=ident[:], scalar1=hf[:, 0:1], scalar2=None, op0=ALU.mult)
+        nc.vector.tensor_tensor(out=hs[:], in0=hsq[:, 0:1], in1=hsq[:, 1:2], op=ALU.add)
+        nc.vector.scalar_tensor_tensor(
+            out=rot[:, 0::2], in0=ident[:, 1::2], scalar=nh1[:], in1=rot_d[:, 0::2], op0=ALU.mult, op1=ALU.add
+        )
+        nc.vector.tensor_scalar(out=flag[:], in0=hs[:], scalar1=0.0, scalar2=None, op0=ALU.is_equal)
+        nc.vector.scalar_tensor_tensor(
+            out=rot[:, 1::2], in0=ident[:, 0::2], scalar=hf[:, 1:2], in1=rot_d[:, 1::2], op0=ALU.mult, op1=ALU.add
+        )
+        nc.vector.scalar_tensor_tensor(
+            out=den[:], in0=hs[:], scalar=64.0, in1=flag[:], op0=ALU.mult, op1=ALU.add
+        )
+        nc.vector.reciprocal(out=inv[:], in_=den[:])
+
+        def weights():
+            nc.vector.tensor_copy(
+                out=w1[:].rearrange("p (t m b) -> p m t b", t=PACK, b=2),
+                in_=w1_raw[:].rearrange("p (m t b) -> p m t b", t=PACK, b=2),
             )
-            nc.vector.tensor_scalar(out=flag[:], in0=hs[:], scalar1=0.0, scalar2=None, op0=ALU.is_equal)
-            nc.vector.scalar_tensor_tensor(
-                out=rot[:, 1::2], in0=ident[:, 0::2], scalar=hf[:, 1:2], in1=rot_d[:, 1::2], op0=ALU.mult, op1=ALU.add
+            nc.vector.tensor_copy(
+                out=s1[:].rearrange("p (t m) -> p m t", t=PACK),
+                in_=s_raw[:, 0:HID].rearrange("p (m t) -> p m t", t=PACK),
             )
-            nc.vector.scalar_tensor_tensor(
-                out=den[:], in0=hs[:], scalar=64.0, in1=flag[:], op0=ALU.mult, op1=ALU.add
-            )
-            nc.vector.reciprocal(out=inv[:], in_=den[:])
 
         st = {}
 
-        def widen(c):
+        def scale_x(c):
             g, j, slots = chunk_home[c]
-            half = slots // 2
             xw = work.tile([P, slots * K1], BF16, name="xw")
-            nc.scalar.copy(
-                out=xw[:, half * K1 :], in_=x_sb[g][:, (j + half) * K1 : (j + slots) * K1].bitcast(E4M3)
+            nc.vector.tensor_tensor(
+                out=xw[:],
+                in0=x_sb[g][:, j * K1 : (j + slots) * K1].bitcast(E4M3),
+                in1=scale_row[:, : slots * K1],
+                op=ALU.mult,
             )
             st["xw", c] = xw
-
-        def widen_v(c):
-            g, j, slots = chunk_home[c]
-            half = slots // 2
-            xw = st["xw", c]
-            nc.vector.tensor_copy(out=xw[:, : half * K1], in_=x_sb[g][:, j * K1 : (j + half) * K1].bitcast(E4M3))
 
         def transposes(c):
             words = st.pop(("xw", c))[:].bitcast(F32)
@@ -178,16 +184,12 @@ def tile_channel_net_pa_w4_kernel(
                 banks.append(xt)
             st["xt", c] = banks
 
-        def scale_x(c):
+        def words_out(c):
             banks = st.pop(("xt", c))
-            xs = work.tile([P, CHUNKS[c], 2, 2], BF16, name="xs", align_bytes=64)
+            xs = work.tile([P, CHUNKS[c] * PACK], BF16, name="xs", align_bytes=64)
+            words = xs[:].bitcast(F32).rearrange("p (n u) -> p n u", u=2)
             for i, xt in enumerate(banks):
-                nc.vector.tensor_tensor(
-                    out=xs[:, i * BANK : (i + 1) * BANK],
-                    in0=xt[:].bitcast(BF16).rearrange("p u (n e) -> p n u e", e=2),
-                    in1=sc[:].rearrange("p (u e) -> p u e", e=2).unsqueeze(1).to_broadcast([P, BANK, 2, 2]),
-                    op=ALU.mult,
-                )
+                nc.scalar.copy(out=words[:, i * BANK : (i + 1) * BANK, :], in_=xt[:].rearrange("p u n -> p n u"))
             st["xs", c] = xs
 
         def quant_x(c):
@@ -195,7 +197,7 @@ def tile_channel_net_pa_w4_kernel(
             xq = work.tile([P, CHUNKS[c]], U32, name="xq", align_bytes=64)
             xqs = work.tile([P, CHUNKS[c]], U8, name="xqs", align_bytes=64)
             nc.vector.quantize_mx(
-                out=xq[:].bitcast(E4M3X4), scales=xqs[:], in_=xs[:].rearrange("p n u e -> p (n u e)")
+                out=xq[:].bitcast(E4M3X4), scales=xqs[:], in_=xs[:]
             )
             st["xq", c] = (xq, xqs)
 
@@ -204,7 +206,7 @@ def tile_channel_net_pa_w4_kernel(
             banks = []
             per = 512 // CHUNKS[c]
             for b in range(PACK // per):
-                bank = psum.tile([P, per, CHUNKS[c]], F32, name="hid", bufs=4)
+                bank = psum.tile([P, per, CHUNKS[c]], F32, name="hid", bufs=3)
                 for i in range(per):
                     t = per * b + i
                     nc.tensor.matmul_mx(
@@ -219,28 +221,24 @@ def tile_channel_net_pa_w4_kernel(
                 banks.append(bank)
             st["hid", c] = banks
 
-        def relu(c):
-            banks = st.pop(("hid", c))
+        def relu(c, half):
+            banks = st["hid", c]
             per = 512 // CHUNKS[c]
-            planes = work.tile([P, PACK, CHUNKS[c]], BF16, name="planes")
-            for t in range(PACK):
+            if half == 0:
+                planes = work.tile([P, PACK, CHUNKS[c]], BF16, name="planes")
+                st["planes", c] = planes
+            planes = st["planes", c]
+            for t in (2 * half, 2 * half + 1):
                 nc.scalar.activation(
                     out=planes[:, t, :], in_=banks[t // per][:, t % per, :], func=ACT.Relu, bias=b1f[:, t : t + 1]
                 )
-            st["planes", c] = planes
 
         def interleave(c):
             planes = st.pop(("planes", c))
-            ai = work.tile([P, CHUNKS[c], PACK], BF16, name="ai", align_bytes=64, bufs=1)
-            for n0 in range(0, CHUNKS[c], BANK):
-                nc.gpsimd.tensor_scalar(
-                    out=ai[:, n0 : n0 + BANK, :],
-                    in0=planes[:, :, n0 : n0 + BANK].rearrange("p t n -> p n t"),
-                    scalar1=1.0,
-                    scalar2=0.0,
-                    op0=ALU.mult,
-                    op1=ALU.add,
-                )
+            ai = work.tile([P, CHUNKS[c], PACK], BF16, name="ai", align_bytes=64)
+            nc.vector.tensor_copy(
+                out=ai[:].rearrange("p (c i) t -> p c t i", i=4), in_=planes[:].rearrange("p t (c i) -> p c t i", i=4)
+            )
             st["ai", c] = ai
 
         def quant_a(c):
@@ -273,7 +271,7 @@ def tile_channel_net_pa_w4_kernel(
         def rotate(c):
             zb = st.pop(("zb", c))
             slots = chunk_home[c][2]
-            r = psum.tile([P, slots, CH], F32, name="r", bufs=1)
+            r = psum.tile([P, slots, CH], F32, name="r", bufs=2)
             for j in range(slots):
                 nc.tensor.matmul(
                     out=r[:, j, :], lhsT=zb[:, j * P : (j + 1) * P], rhs=rot[:], start=True, stop=True
@@ -313,25 +311,25 @@ def tile_channel_net_pa_w4_kernel(
 
         n = len(CHUNKS)
         order = [
-            (finish, 4),
-            (second_matmul, 2),
-            (relu, 0),
-            (rotate, 3),
-            (bias_z, 2),
-            (norms, 3),
-            (transposes, -2),
-            (scale_x, -1),
-            (widen, -3),
-            (widen_v, -3),
-            (quant_x, -1),
-            (interleave, 1),
-            (quant_a, 1),
-            (first_matmul, -1),
+            (lambda c: relu(c, 0), 4),
+            (quant_x, 3),
+            (lambda c: relu(c, 1), 4),
+            (second_matmul, 9),
+            (interleave, 7),
+            (quant_a, 8),
+            (bias_z, 9),
+            (transposes, 1),
+            (scale_x, 0),
+            (finish, 11),
+            (rotate, 10),
+            (first_matmul, 3),
+            (words_out, 1),
+            (norms, 10),
         ]
         with tc.manual_schedule():
-            for s in range(-3, n + 5):
-                if s == 0:
-                    late_constants()
+            for s in range(n + 12):
+                if s == 2:
+                    weights()
                 for stage, lag in order:
                     c = s - lag
                     if 0 <= c < n:

@@ -21,8 +21,8 @@ HID = 512
 CH = 128
 PACK = 4
 
-CHUNKS = [256, 256] + [512] * 14 + [256, 256]
-GROUPS = [[256], [256], [512]] + [[512, 512]] * 6 + [[512, 256, 256]]
+CHUNKS = [256] * 4 + [512] * 12 + [256] * 4
+GROUPS = [[256], [256], [256, 256]] + [[512, 512]] * 6 + [[256] * 4]
 BANK = 256
 
 FLOPS = 2 * TOKENS * HID * (K1 + CH)
@@ -77,9 +77,15 @@ def tile_channel_net_pa_w4_kernel(
         h_raw = const.tile([P, 2], BF16, name="h_raw")
         hf = const.tile([P, 2], F32, name="hf")
         ident = const.tile([P, P], F32, name="ident")
+        perm = const.tile([P, P], F32, name="perm")
         rot = const.tile([P, P], F32, name="rot")
         rot_d = const.tile([P, P], F32, name="rot_d")
         nh1 = const.tile([P, 1], F32, name="nh1")
+        even = const.tile([P, 1], F32, name="even")
+        sign = const.tile([P, 1], F32, name="sign")
+        sh1 = const.tile([P, 1], F32, name="sh1")
+        h0b2 = const.tile([P, 1], F32, name="h0b2")
+        sh1b2 = const.tile([P, 1], F32, name="sh1b2")
         hsq = const.tile([P, 2], F32, name="hsq")
         hs = const.tile([P, 1], F32, name="hs")
         flag = const.tile([P, 1], F32, name="flag")
@@ -96,8 +102,8 @@ def tile_channel_net_pa_w4_kernel(
         nc.scalar.dma_start(out=h_raw[:], in_=h.partition_broadcast(P))
         nc.scalar.dma_start(out=b2_raw[:], in_=b2.rearrange("(p o) -> p o", o=1))
         nc.scalar.dma_start(out=b1_raw[:], in_=b1.rearrange("(p t) -> p t", t=PACK))
-        load_x(0)
         nc.sync.dma_start(out=w1_raw[:], in_=W1_words[0])
+        load_x(0)
         for q in range(4):
             nc.sync.dma_start(
                 out=s_raw[32 * q : 32 * q + 4, 0:HID].bitcast(I32),
@@ -111,12 +117,48 @@ def tile_channel_net_pa_w4_kernel(
                 out=s_raw[32 * q : 32 * q + 4, HID : HID + CH].bitcast(I32),
                 in_=W2_scales[0, 4 * q : 4 * q + 4, :].bitcast(I32),
             )
+        load_x(3)
         load_noise(0)
         load_noise(1)
         load_noise(2)
-        for g in range(3, len(GROUPS)):
+        load_x(4)
+        load_noise(3)
+        for g in range(5, len(GROUPS)):
             load_x(g)
-            load_noise(g)
+            load_noise(g - 1)
+        load_noise(len(GROUPS) - 1)
+
+        nc.vector.tensor_copy(out=b1f[:], in_=b1_raw[:])
+
+        nc.vector.tensor_copy(out=b2f[:], in_=b2_raw[:])
+        nc.vector.tensor_copy(out=hf[:], in_=h_raw[:])
+        nc.vector.tensor_tensor(out=hsq[:], in0=hf[:], in1=hf[:], op=ALU.mult)
+        nc.vector.tensor_copy(out=perm[:, 0::2], in_=ident[:, 1::2])
+        nc.vector.tensor_tensor(out=hs[:], in0=hsq[:, 0:1], in1=hsq[:, 1:2], op=ALU.add)
+        nc.vector.tensor_copy(out=perm[:, 1::2], in_=ident[:, 0::2])
+        nc.vector.reduce_sum(out=even[:], in_=ident[:, 0::2], axis=mybir.AxisListType.X)
+        nc.vector.tensor_scalar(out=flag[:], in0=hs[:], scalar1=0.0, scalar2=None, op0=ALU.is_equal)
+        nc.vector.tensor_scalar(out=sign[:], in0=even[:], scalar1=2.0, scalar2=-1.0, op0=ALU.mult, op1=ALU.add)
+        nc.vector.scalar_tensor_tensor(
+            out=den[:], in0=hs[:], scalar=64.0, in1=flag[:], op0=ALU.mult, op1=ALU.add
+        )
+        nc.vector.tensor_tensor(out=sh1[:], in0=sign[:], in1=hf[:, 1:2], op=ALU.mult)
+        nc.vector.reciprocal(out=inv[:], in_=den[:])
+        nc.vector.tensor_tensor(out=h0b2[:], in0=b2f[:], in1=hf[:, 0:1], op=ALU.mult)
+        nc.vector.tensor_scalar(out=nh1[:], in0=hf[:, 1:2], scalar1=-1.0, scalar2=None, op0=ALU.mult)
+        nc.vector.tensor_scalar(out=rot_d[:], in0=ident[:], scalar1=hf[:, 0:1], scalar2=None, op0=ALU.mult)
+        nc.vector.tensor_tensor(out=sh1b2[:], in0=b2f[:], in1=sh1[:], op=ALU.mult)
+        nc.vector.scalar_tensor_tensor(
+            out=rot[:, 0::2], in0=perm[:, 0::2], scalar=nh1[:], in1=rot_d[:, 0::2], op0=ALU.mult, op1=ALU.add
+        )
+        nc.vector.scalar_tensor_tensor(
+            out=rot[:, 1::2], in0=perm[:, 1::2], scalar=hf[:, 1:2], in1=rot_d[:, 1::2], op0=ALU.mult, op1=ALU.add
+        )
+
+        nc.vector.tensor_copy(
+            out=w1[:].rearrange("p (t m b) -> p m t b", t=PACK, b=2),
+            in_=w1_raw[:].rearrange("p (m t b) -> p m t b", t=PACK, b=2),
+        )
 
         scale_ps = psum.tile([P, 2, BANK], F32, name="xt", bufs=2)
         scale_flat = scale_ps[:].rearrange("p u n -> p (u n)")
@@ -126,31 +168,7 @@ def tile_channel_net_pa_w4_kernel(
         for i in range(1, 4):
             nc.scalar.copy(out=scale_row[:, i * K1 : (i + 1) * K1], in_=scale_flat)
 
-        nc.vector.tensor_copy(out=b1f[:], in_=b1_raw[:])
-
-        nc.vector.tensor_copy(out=b2f[:], in_=b2_raw[:])
-        nc.vector.tensor_copy(out=hf[:], in_=h_raw[:])
-        nc.vector.tensor_scalar(out=nh1[:], in0=hf[:, 1:2], scalar1=-1.0, scalar2=None, op0=ALU.mult)
-        nc.vector.tensor_tensor(out=hsq[:], in0=hf[:], in1=hf[:], op=ALU.mult)
-        nc.vector.tensor_scalar(out=rot_d[:], in0=ident[:], scalar1=hf[:, 0:1], scalar2=None, op0=ALU.mult)
-        nc.vector.tensor_tensor(out=hs[:], in0=hsq[:, 0:1], in1=hsq[:, 1:2], op=ALU.add)
-        nc.vector.scalar_tensor_tensor(
-            out=rot[:, 0::2], in0=ident[:, 1::2], scalar=nh1[:], in1=rot_d[:, 0::2], op0=ALU.mult, op1=ALU.add
-        )
-        nc.vector.tensor_scalar(out=flag[:], in0=hs[:], scalar1=0.0, scalar2=None, op0=ALU.is_equal)
-        nc.vector.scalar_tensor_tensor(
-            out=rot[:, 1::2], in0=ident[:, 0::2], scalar=hf[:, 1:2], in1=rot_d[:, 1::2], op0=ALU.mult, op1=ALU.add
-        )
-        nc.vector.scalar_tensor_tensor(
-            out=den[:], in0=hs[:], scalar=64.0, in1=flag[:], op0=ALU.mult, op1=ALU.add
-        )
-        nc.vector.reciprocal(out=inv[:], in_=den[:])
-
-        def weights():
-            nc.vector.tensor_copy(
-                out=w1[:].rearrange("p (t m b) -> p m t b", t=PACK, b=2),
-                in_=w1_raw[:].rearrange("p (m t b) -> p m t b", t=PACK, b=2),
-            )
+        def weight_scales():
             nc.vector.tensor_copy(
                 out=s1[:].rearrange("p (t m) -> p m t", t=PACK),
                 in_=s_raw[:, 0:HID].rearrange("p (m t) -> p m t", t=PACK),
@@ -221,14 +239,12 @@ def tile_channel_net_pa_w4_kernel(
                 banks.append(bank)
             st["hid", c] = banks
 
-        def relu(c, half):
-            banks = st["hid", c]
+        def relu(c):
+            banks = st.pop(("hid", c))
             per = 512 // CHUNKS[c]
-            if half == 0:
-                planes = work.tile([P, PACK, CHUNKS[c]], BF16, name="planes")
-                st["planes", c] = planes
-            planes = st["planes", c]
-            for t in (2 * half, 2 * half + 1):
+            planes = work.tile([P, PACK, CHUNKS[c]], BF16, name="planes")
+            st["planes", c] = planes
+            for t in range(PACK):
                 nc.scalar.activation(
                     out=planes[:, t, :], in_=banks[t // per][:, t % per, :], func=ACT.Relu, bias=b1f[:, t : t + 1]
                 )
@@ -264,17 +280,30 @@ def tile_channel_net_pa_w4_kernel(
 
         def bias_z(c):
             z = st.pop(("z", c))
-            zb = work.tile([P, CHUNKS[c]], F32, name="zb")
-            nc.scalar.activation(out=zb[:], in_=z[:], func=ACT.Identity, bias=b2f[:])
-            st["zb", c] = zb
+            half = CHUNKS[c] // 2
+            zb = work.tile([P, half], F32, name="zb")
+            za = work.tile([P, half], F32, name="za")
+            zc = work.tile([P, half], F32, name="zc")
+            nc.scalar.activation(out=zb[:], in_=z[:, :half], func=ACT.Identity, bias=b2f[:])
+            nc.scalar.activation(out=za[:], in_=z[:, half:], func=ACT.Identity, scale=hf[:, 0:1], bias=h0b2[:])
+            nc.scalar.activation(out=zc[:], in_=z[:, half:], func=ACT.Identity, scale=sh1[:], bias=sh1b2[:])
+            st["zb", c] = (zb, za, zc)
 
         def rotate(c):
-            zb = st.pop(("zb", c))
+            zb, za, zc = st.pop(("zb", c))
             slots = chunk_home[c][2]
             r = psum.tile([P, slots, CH], F32, name="r", bufs=2)
-            for j in range(slots):
+            half = slots // 2
+            for j in range(half):
+                cols = slice(j * P, (j + 1) * P)
+                nc.tensor.matmul(out=r[:, j, :], lhsT=zb[:, cols], rhs=rot[:], start=True, stop=True)
+            for j in range(half):
+                cols = slice(j * P, (j + 1) * P)
                 nc.tensor.matmul(
-                    out=r[:, j, :], lhsT=zb[:, j * P : (j + 1) * P], rhs=rot[:], start=True, stop=True
+                    out=r[:, half + j, :], lhsT=za[:, cols], rhs=ident[:], is_transpose=True, start=True, stop=False
+                )
+                nc.tensor.matmul(
+                    out=r[:, half + j, :], lhsT=zc[:, cols], rhs=perm[:], is_transpose=True, start=False, stop=True
                 )
             st["r", c] = r
 
@@ -311,25 +340,24 @@ def tile_channel_net_pa_w4_kernel(
 
         n = len(CHUNKS)
         order = [
-            (lambda c: relu(c, 0), 4),
             (quant_x, 3),
-            (lambda c: relu(c, 1), 4),
             (second_matmul, 9),
+            (rotate, 11),
             (interleave, 7),
-            (quant_a, 8),
+            (relu, 4),
             (bias_z, 9),
             (transposes, 1),
+            (quant_a, 8),
+            (finish, 12),
             (scale_x, 0),
-            (finish, 11),
-            (rotate, 10),
             (first_matmul, 3),
+            (norms, 11),
             (words_out, 1),
-            (norms, 10),
         ]
         with tc.manual_schedule():
-            for s in range(n + 12):
-                if s == 2:
-                    weights()
+            for s in range(n + 13):
+                if s == 1:
+                    weight_scales()
                 for stage, lag in order:
                     c = s - lag
                     if 0 <= c < n:

@@ -21,8 +21,8 @@ HID = 512
 CH = 128
 PACK = 4
 
-CHUNKS = [256] * 4 + [512] * 12 + [256] * 4
-GROUPS = [[256], [256], [256, 256]] + [[512, 512]] * 6 + [[256] * 4]
+CHUNKS = [256] * 2 + [512] * 13 + [256] * 4
+GROUPS = [[256], [256], [512]] + [[512, 512]] * 6 + [[256] * 4]
 BANK = 256
 
 FLOPS = 2 * TOKENS * HID * (K1 + CH)
@@ -64,7 +64,6 @@ def tile_channel_net_pa_w4_kernel(
             nc.sync.dma_start(out=nt[:], in_=noise[b : b + size, :].rearrange("(p j) n -> p j n", j=slots))
 
         sc = const.tile([P, PACK], F32, name="sc")
-        scale_row = const.tile([P, 4 * K1], F32, name="scale_row")
         w1_raw = const.tile([P, HID * 2], U8, name="w1_raw")
         w1 = const.tile([P, HID * 2], U8, name="w1", align_bytes=64)
         s_raw = const.tile([P, HID + CH], U8, name="s_raw", align_bytes=64)
@@ -81,11 +80,6 @@ def tile_channel_net_pa_w4_kernel(
         rot = const.tile([P, P], F32, name="rot")
         rot_d = const.tile([P, P], F32, name="rot_d")
         nh1 = const.tile([P, 1], F32, name="nh1")
-        even = const.tile([P, 1], F32, name="even")
-        sign = const.tile([P, 1], F32, name="sign")
-        sh1 = const.tile([P, 1], F32, name="sh1")
-        h0b2 = const.tile([P, 1], F32, name="h0b2")
-        sh1b2 = const.tile([P, 1], F32, name="sh1b2")
         hsq = const.tile([P, 2], F32, name="hsq")
         hs = const.tile([P, 1], F32, name="hs")
         flag = const.tile([P, 1], F32, name="flag")
@@ -98,7 +92,7 @@ def tile_channel_net_pa_w4_kernel(
         make_identity(nc, ident[:])
         nc.scalar.activation(out=warm[:], in_=warm[:], func=ACT.Abs_reciprocal_sqrt)
 
-        nc.scalar.dma_start(out=sc[:], in_=x_scale.rearrange("o (t p) -> p (o t)", t=PACK))
+        nc.scalar.dma_start(out=sc[:], in_=x_scale.rearrange("o (p t) -> p (o t)", t=PACK))
         nc.scalar.dma_start(out=h_raw[:], in_=h.partition_broadcast(P))
         nc.scalar.dma_start(out=b2_raw[:], in_=b2.rearrange("(p o) -> p o", o=1))
         nc.scalar.dma_start(out=b1_raw[:], in_=b1.rearrange("(p t) -> p t", t=PACK))
@@ -136,18 +130,13 @@ def tile_channel_net_pa_w4_kernel(
         nc.vector.tensor_copy(out=perm[:, 0::2], in_=ident[:, 1::2])
         nc.vector.tensor_tensor(out=hs[:], in0=hsq[:, 0:1], in1=hsq[:, 1:2], op=ALU.add)
         nc.vector.tensor_copy(out=perm[:, 1::2], in_=ident[:, 0::2])
-        nc.vector.reduce_sum(out=even[:], in_=ident[:, 0::2], axis=mybir.AxisListType.X)
         nc.vector.tensor_scalar(out=flag[:], in0=hs[:], scalar1=0.0, scalar2=None, op0=ALU.is_equal)
-        nc.vector.tensor_scalar(out=sign[:], in0=even[:], scalar1=2.0, scalar2=-1.0, op0=ALU.mult, op1=ALU.add)
         nc.vector.scalar_tensor_tensor(
             out=den[:], in0=hs[:], scalar=64.0, in1=flag[:], op0=ALU.mult, op1=ALU.add
         )
-        nc.vector.tensor_tensor(out=sh1[:], in0=sign[:], in1=hf[:, 1:2], op=ALU.mult)
         nc.vector.reciprocal(out=inv[:], in_=den[:])
-        nc.vector.tensor_tensor(out=h0b2[:], in0=b2f[:], in1=hf[:, 0:1], op=ALU.mult)
         nc.vector.tensor_scalar(out=nh1[:], in0=hf[:, 1:2], scalar1=-1.0, scalar2=None, op0=ALU.mult)
         nc.vector.tensor_scalar(out=rot_d[:], in0=ident[:], scalar1=hf[:, 0:1], scalar2=None, op0=ALU.mult)
-        nc.vector.tensor_tensor(out=sh1b2[:], in0=b2f[:], in1=sh1[:], op=ALU.mult)
         nc.vector.scalar_tensor_tensor(
             out=rot[:, 0::2], in0=perm[:, 0::2], scalar=nh1[:], in1=rot_d[:, 0::2], op0=ALU.mult, op1=ALU.add
         )
@@ -160,14 +149,6 @@ def tile_channel_net_pa_w4_kernel(
             in_=w1_raw[:].rearrange("p (m t b) -> p m t b", t=PACK, b=2),
         )
 
-        scale_ps = psum.tile([P, 2, BANK], F32, name="xt", bufs=2)
-        scale_flat = scale_ps[:].rearrange("p u n -> p (u n)")
-        for t in range(PACK):
-            nc.tensor.transpose(scale_flat[:, t * P : (t + 1) * P], sc[:, t : t + 1].to_broadcast([P, P]), ident[:])
-        nc.vector.tensor_copy(out=scale_row[:, 0:K1], in_=scale_flat)
-        for i in range(1, 4):
-            nc.scalar.copy(out=scale_row[:, i * K1 : (i + 1) * K1], in_=scale_flat)
-
         def weight_scales():
             nc.vector.tensor_copy(
                 out=s1[:].rearrange("p (t m) -> p m t", t=PACK),
@@ -176,16 +157,19 @@ def tile_channel_net_pa_w4_kernel(
 
         st = {}
 
-        def scale_x(c):
+        def widen(c):
             g, j, slots = chunk_home[c]
+            x = x_sb[g][:, j * K1 : (j + slots) * K1].bitcast(E4M3)
+            split = slots * K1 // (2 if c < 3 else 4)
             xw = work.tile([P, slots * K1], BF16, name="xw")
-            nc.vector.tensor_tensor(
-                out=xw[:],
-                in0=x_sb[g][:, j * K1 : (j + slots) * K1].bitcast(E4M3),
-                in1=scale_row[:, : slots * K1],
-                op=ALU.mult,
-            )
+            nc.scalar.copy(out=xw[:, split:], in_=x[:, split:])
             st["xw", c] = xw
+
+        def widen_v(c):
+            g, j, slots = chunk_home[c]
+            x = x_sb[g][:, j * K1 : (j + slots) * K1].bitcast(E4M3)
+            split = slots * K1 // (2 if c < 3 else 4)
+            nc.vector.tensor_copy(out=st["xw", c][:, :split], in_=x[:, :split])
 
         def transposes(c):
             words = st.pop(("xw", c))[:].bitcast(F32)
@@ -202,12 +186,16 @@ def tile_channel_net_pa_w4_kernel(
                 banks.append(xt)
             st["xt", c] = banks
 
-        def words_out(c):
+        def scale_x(c):
             banks = st.pop(("xt", c))
-            xs = work.tile([P, CHUNKS[c] * PACK], BF16, name="xs", align_bytes=64)
-            words = xs[:].bitcast(F32).rearrange("p (n u) -> p n u", u=2)
+            xs = work.tile([P, CHUNKS[c], 2, 2], BF16, name="xs", align_bytes=64)
             for i, xt in enumerate(banks):
-                nc.scalar.copy(out=words[:, i * BANK : (i + 1) * BANK, :], in_=xt[:].rearrange("p u n -> p n u"))
+                nc.vector.tensor_tensor(
+                    out=xs[:, i * BANK : (i + 1) * BANK],
+                    in0=xt[:].bitcast(BF16).rearrange("p u (n e) -> p n u e", e=2),
+                    in1=sc[:].rearrange("p (u e) -> p u e", e=2).unsqueeze(1).to_broadcast([P, BANK, 2, 2]),
+                    op=ALU.mult,
+                )
             st["xs", c] = xs
 
         def quant_x(c):
@@ -215,7 +203,7 @@ def tile_channel_net_pa_w4_kernel(
             xq = work.tile([P, CHUNKS[c]], U32, name="xq", align_bytes=64)
             xqs = work.tile([P, CHUNKS[c]], U8, name="xqs", align_bytes=64)
             nc.vector.quantize_mx(
-                out=xq[:].bitcast(E4M3X4), scales=xqs[:], in_=xs[:]
+                out=xq[:].bitcast(E4M3X4), scales=xqs[:], in_=xs[:].rearrange("p n u e -> p (n u e)")
             )
             st["xq", c] = (xq, xqs)
 
@@ -251,9 +239,9 @@ def tile_channel_net_pa_w4_kernel(
 
         def interleave(c):
             planes = st.pop(("planes", c))
-            ai = work.tile([P, CHUNKS[c], PACK], BF16, name="ai", align_bytes=64)
-            nc.vector.tensor_copy(
-                out=ai[:].rearrange("p (c i) t -> p c t i", i=4), in_=planes[:].rearrange("p t (c i) -> p c t i", i=4)
+            ai = work.tile([P, CHUNKS[c], PACK], BF16, name="ai", align_bytes=64, bufs=3)
+            nc.gpsimd.tensor_scalar(
+                out=ai[:], in0=planes[:].rearrange("p t n -> p n t"), scalar1=1.0, scalar2=0.0, op0=ALU.mult, op1=ALU.add
             )
             st["ai", c] = ai
 
@@ -280,31 +268,16 @@ def tile_channel_net_pa_w4_kernel(
 
         def bias_z(c):
             z = st.pop(("z", c))
-            half = CHUNKS[c] // 2
-            zb = work.tile([P, half], F32, name="zb")
-            za = work.tile([P, half], F32, name="za")
-            zc = work.tile([P, half], F32, name="zc")
-            nc.scalar.activation(out=zb[:], in_=z[:, :half], func=ACT.Identity, bias=b2f[:])
-            nc.scalar.activation(out=za[:], in_=z[:, half:], func=ACT.Identity, scale=hf[:, 0:1], bias=h0b2[:])
-            nc.scalar.activation(out=zc[:], in_=z[:, half:], func=ACT.Identity, scale=sh1[:], bias=sh1b2[:])
-            st["zb", c] = (zb, za, zc)
+            zb = work.tile([P, CHUNKS[c]], F32, name="zb")
+            nc.scalar.activation(out=zb[:], in_=z[:], func=ACT.Identity, bias=b2f[:])
+            st["zb", c] = zb
 
         def rotate(c):
-            zb, za, zc = st.pop(("zb", c))
+            zb = st.pop(("zb", c))
             slots = chunk_home[c][2]
             r = psum.tile([P, slots, CH], F32, name="r", bufs=2)
-            half = slots // 2
-            for j in range(half):
-                cols = slice(j * P, (j + 1) * P)
-                nc.tensor.matmul(out=r[:, j, :], lhsT=zb[:, cols], rhs=rot[:], start=True, stop=True)
-            for j in range(half):
-                cols = slice(j * P, (j + 1) * P)
-                nc.tensor.matmul(
-                    out=r[:, half + j, :], lhsT=za[:, cols], rhs=ident[:], is_transpose=True, start=True, stop=False
-                )
-                nc.tensor.matmul(
-                    out=r[:, half + j, :], lhsT=zc[:, cols], rhs=perm[:], is_transpose=True, start=False, stop=True
-                )
+            for j in range(slots):
+                nc.tensor.matmul(out=r[:, j, :], lhsT=zb[:, j * P : (j + 1) * P], rhs=rot[:], start=True, stop=True)
             st["r", c] = r
 
         def norms(c):
@@ -340,22 +313,23 @@ def tile_channel_net_pa_w4_kernel(
 
         n = len(CHUNKS)
         order = [
-            (quant_x, 3),
+            (finish, 13),
+            (interleave, 8),
+            (relu, 5),
             (second_matmul, 9),
-            (rotate, 11),
-            (interleave, 7),
-            (relu, 4),
-            (bias_z, 9),
-            (transposes, 1),
+            (scale_x, 4),
             (quant_a, 8),
-            (finish, 12),
-            (scale_x, 0),
-            (first_matmul, 3),
+            (rotate, 11),
+            (widen, 0),
+            (transposes, 3),
+            (quant_x, 4),
+            (bias_z, 9),
+            (first_matmul, 4),
+            (widen_v, 0),
             (norms, 11),
-            (words_out, 1),
         ]
         with tc.manual_schedule():
-            for s in range(n + 13):
+            for s in range(n + 14):
                 if s == 1:
                     weight_scales()
                 for stage, lag in order:

from contextlib import ExitStack

import concourse.mybir as mybir
from concourse.masks import make_identity

F32 = mybir.dt.float32
BF16 = mybir.dt.bfloat16
I32 = mybir.dt.int32
U32 = mybir.dt.uint32
U8 = mybir.dt.uint8
E4M3 = mybir.dt.float8_e4m3fn
E4M3X4 = mybir.dt.float8_e4m3fn_x4
E2M1X4 = mybir.dt.float4_e2m1fn_x4
ACT = mybir.ActivationFunctionType
ALU = mybir.AluOpType

P = 128
TOKENS = 8192
K1 = 512
HID = 512
CH = 128
PACK = 4

CHUNKS = [256] * 2 + [512] * 13 + [256] * 4
GROUPS = [[256], [256], [512]] + [[512, 512]] * 6 + [[256] * 4]
BANK = 256

FLOPS = 2 * TOKENS * HID * (K1 + CH)


def tile_channel_net_pa_w4_kernel(
    tc, x_bytes, x_scale, noise, h, W1_words, W1_scales, b1, W2_words, W2_scales, b2, out
):
    nc = tc.nc
    with ExitStack() as ctx:
        const = ctx.enter_context(tc.tile_pool(name="const", bufs=1))
        data = ctx.enter_context(tc.tile_pool(name="data", bufs=1))
        work = ctx.enter_context(tc.tile_pool(name="work", bufs=4))
        psum = ctx.enter_context(tc.psum_pool(name="psum", bufs=1))

        x_sb, noise_sb, chunk_home = [], [], []
        base = 0
        loads = []
        for g, parts in enumerate(GROUPS):
            size = sum(parts)
            slots = size // P
            xt = data.tile([P, slots * K1], U8, name="x_%d" % g)
            nt = data.tile([P, slots, CH], BF16, name="noise_%d" % g)
            x_sb.append(xt)
            noise_sb.append(nt)
            loads.append((xt, nt, base, size, slots))
            j = 0
            for part in parts:
                chunk_home.append((g, j, part // P))
                j += part // P
            base += size

        def load_x(g):
            xt, nt, b, size, slots = loads[g]
            nc.sync.dma_start(out=xt[:], in_=x_bytes[b : b + size, :].rearrange("(p j) k -> p (j k)", j=slots))

        def load_noise(g):
            xt, nt, b, size, slots = loads[g]
            nc.sync.dma_start(out=nt[:], in_=noise[b : b + size, :].rearrange("(p j) n -> p j n", j=slots))

        sc = const.tile([P, PACK], F32, name="sc")
        w1_raw = const.tile([P, HID * 2], U8, name="w1_raw")
        w1 = const.tile([P, HID * 2], U8, name="w1", align_bytes=64)
        s_raw = const.tile([P, HID + CH], U8, name="s_raw", align_bytes=64)
        s1 = const.tile([P, HID], U8, name="s1", align_bytes=64)
        w2 = const.tile([P, CH * 2], U8, name="w2", align_bytes=64)
        b1_raw = const.tile([P, PACK], BF16, name="b1_raw")
        b1f = const.tile([P, PACK], F32, name="b1f")
        b2_raw = const.tile([P, 1], BF16, name="b2_raw")
        b2f = const.tile([P, 1], F32, name="b2f")
        h_raw = const.tile([P, 2], BF16, name="h_raw")
        hf = const.tile([P, 2], F32, name="hf")
        ident = const.tile([P, P], F32, name="ident")
        perm = const.tile([P, P], F32, name="perm")
        rot = const.tile([P, P], F32, name="rot")
        rot_d = const.tile([P, P], F32, name="rot_d")
        nh1 = const.tile([P, 1], F32, name="nh1")
        hsq = const.tile([P, 2], F32, name="hsq")
        hs = const.tile([P, 1], F32, name="hs")
        flag = const.tile([P, 1], F32, name="flag")
        den = const.tile([P, 1], F32, name="den")
        inv = const.tile([P, 1], F32, name="inv")
        warm = const.tile([P, 1], F32, name="warm")

        nc.vector.memset(s_raw[:].bitcast(I32), 0)
        nc.vector.memset(warm[:], 1.0)
        make_identity(nc, ident[:])
        nc.scalar.activation(out=warm[:], in_=warm[:], func=ACT.Abs_reciprocal_sqrt)

        nc.scalar.dma_start(out=sc[:], in_=x_scale.rearrange("o (p t) -> p (o t)", t=PACK))
        nc.scalar.dma_start(out=h_raw[:], in_=h.partition_broadcast(P))
        nc.scalar.dma_start(out=b2_raw[:], in_=b2.rearrange("(p o) -> p o", o=1))
        nc.scalar.dma_start(out=b1_raw[:], in_=b1.rearrange("(p t) -> p t", t=PACK))
        nc.sync.dma_start(out=w1_raw[:], in_=W1_words[0])
        load_x(0)
        for q in range(4):
            nc.sync.dma_start(
                out=s_raw[32 * q : 32 * q + 4, 0:HID].bitcast(I32),
                in_=W1_scales[0, 4 * q : 4 * q + 4, :].bitcast(I32),
            )
        load_x(1)
        load_x(2)
        nc.sync.dma_start(out=w2[:], in_=W2_words[0])
        for q in range(4):
            nc.sync.dma_start(
                out=s_raw[32 * q : 32 * q + 4, HID : HID + CH].bitcast(I32),
                in_=W2_scales[0, 4 * q : 4 * q + 4, :].bitcast(I32),
            )
        load_x(3)
        load_noise(0)
        load_noise(1)
        load_noise(2)
        load_x(4)
        load_noise(3)
        for g in range(5, len(GROUPS)):
            load_x(g)
            load_noise(g - 1)
        load_noise(len(GROUPS) - 1)

        nc.vector.tensor_copy(out=b1f[:], in_=b1_raw[:])

        nc.vector.tensor_copy(out=b2f[:], in_=b2_raw[:])
        nc.vector.tensor_copy(out=hf[:], in_=h_raw[:])
        nc.vector.tensor_tensor(out=hsq[:], in0=hf[:], in1=hf[:], op=ALU.mult)
        nc.vector.tensor_copy(out=perm[:, 0::2], in_=ident[:, 1::2])
        nc.vector.tensor_tensor(out=hs[:], in0=hsq[:, 0:1], in1=hsq[:, 1:2], op=ALU.add)
        nc.vector.tensor_copy(out=perm[:, 1::2], in_=ident[:, 0::2])
        nc.vector.tensor_scalar(out=flag[:], in0=hs[:], scalar1=0.0, scalar2=None, op0=ALU.is_equal)
        nc.vector.scalar_tensor_tensor(
            out=den[:], in0=hs[:], scalar=64.0, in1=flag[:], op0=ALU.mult, op1=ALU.add
        )
        nc.vector.reciprocal(out=inv[:], in_=den[:])
        nc.vector.tensor_scalar(out=nh1[:], in0=hf[:, 1:2], scalar1=-1.0, scalar2=None, op0=ALU.mult)
        nc.vector.tensor_scalar(out=rot_d[:], in0=ident[:], scalar1=hf[:, 0:1], scalar2=None, op0=ALU.mult)
        nc.vector.scalar_tensor_tensor(
            out=rot[:, 0::2], in0=perm[:, 0::2], scalar=nh1[:], in1=rot_d[:, 0::2], op0=ALU.mult, op1=ALU.add
        )
        nc.vector.scalar_tensor_tensor(
            out=rot[:, 1::2], in0=perm[:, 1::2], scalar=hf[:, 1:2], in1=rot_d[:, 1::2], op0=ALU.mult, op1=ALU.add
        )

        nc.vector.tensor_copy(
            out=w1[:].rearrange("p (t m b) -> p m t b", t=PACK, b=2),
            in_=w1_raw[:].rearrange("p (m t b) -> p m t b", t=PACK, b=2),
        )

        def weight_scales():
            nc.vector.tensor_copy(
                out=s1[:].rearrange("p (t m) -> p m t", t=PACK),
                in_=s_raw[:, 0:HID].rearrange("p (m t) -> p m t", t=PACK),
            )

        st = {}

        def widen(c):
            g, j, slots = chunk_home[c]
            x = x_sb[g][:, j * K1 : (j + slots) * K1].bitcast(E4M3)
            split = slots * K1 // (2 if c < 3 else 4)
            xw = work.tile([P, slots * K1], BF16, name="xw")
            nc.scalar.copy(out=xw[:, split:], in_=x[:, split:])
            st["xw", c] = xw

        def widen_v(c):
            g, j, slots = chunk_home[c]
            x = x_sb[g][:, j * K1 : (j + slots) * K1].bitcast(E4M3)
            split = slots * K1 // (2 if c < 3 else 4)
            nc.vector.tensor_copy(out=st["xw", c][:, :split], in_=x[:, :split])

        def transposes(c):
            words = st.pop(("xw", c))[:].bitcast(F32)
            banks = []
            for j0 in range(0, chunk_home[c][2], 2):
                xt = psum.tile([P, 2, BANK], F32, name="xt", bufs=2)
                for j in range(2):
                    for u in range(2):
                        nc.tensor.transpose(
                            xt[:, u, j * P : (j + 1) * P],
                            words[:, 256 * (j0 + j) + u : 256 * (j0 + j + 1) : 2],
                            ident[:],
                        )
                banks.append(xt)
            st["xt", c] = banks

        def scale_x(c):
            banks = st.pop(("xt", c))
            xs = work.tile([P, CHUNKS[c], 2, 2], BF16, name="xs", align_bytes=64)
            for i, xt in enumerate(banks):
                nc.vector.tensor_tensor(
                    out=xs[:, i * BANK : (i + 1) * BANK],
                    in0=xt[:].bitcast(BF16).rearrange("p u (n e) -> p n u e", e=2),
                    in1=sc[:].rearrange("p (u e) -> p u e", e=2).unsqueeze(1).to_broadcast([P, BANK, 2, 2]),
                    op=ALU.mult,
                )
            st["xs", c] = xs

        def quant_x(c):
            xs = st.pop(("xs", c))
            xq = work.tile([P, CHUNKS[c]], U32, name="xq", align_bytes=64)
            xqs = work.tile([P, CHUNKS[c]], U8, name="xqs", align_bytes=64)
            nc.vector.quantize_mx(
                out=xq[:].bitcast(E4M3X4), scales=xqs[:], in_=xs[:].rearrange("p n u e -> p (n u e)")
            )
            st["xq", c] = (xq, xqs)

        def first_matmul(c):
            xq, xqs = st.pop(("xq", c))
            banks = []
            per = 512 // CHUNKS[c]
            for b in range(PACK // per):
                bank = psum.tile([P, per, CHUNKS[c]], F32, name="hid", bufs=3)
                for i in range(per):
                    t = per * b + i
                    nc.tensor.matmul_mx(
                        out=bank[:, i, :],
                        lhsT=w1[:, 256 * t : 256 * (t + 1)].bitcast(E2M1X4),
                        lhsT_scale=s1[:, P * t : P * (t + 1)],
                        rhs=xq[:].bitcast(E4M3X4),
                        rhs_scale=xqs[:],
                        start=True,
                        stop=True,
                    )
                banks.append(bank)
            st["hid", c] = banks

        def relu(c):
            banks = st.pop(("hid", c))
            per = 512 // CHUNKS[c]
            planes = work.tile([P, PACK, CHUNKS[c]], BF16, name="planes")
            st["planes", c] = planes
            for t in range(PACK):
                nc.scalar.activation(
                    out=planes[:, t, :], in_=banks[t // per][:, t % per, :], func=ACT.Relu, bias=b1f[:, t : t + 1]
                )

        def interleave(c):
            planes = st.pop(("planes", c))
            ai = work.tile([P, CHUNKS[c], PACK], BF16, name="ai", align_bytes=64, bufs=3)
            nc.gpsimd.tensor_scalar(
                out=ai[:], in0=planes[:].rearrange("p t n -> p n t"), scalar1=1.0, scalar2=0.0, op0=ALU.mult, op1=ALU.add
            )
            st["ai", c] = ai

        def quant_a(c):
            ai = st.pop(("ai", c))
            aq = work.tile([P, CHUNKS[c]], U32, name="aq", align_bytes=64)
            aqs = work.tile([P, CHUNKS[c]], U8, name="aqs", align_bytes=64)
            nc.vector.quantize_mx(out=aq[:].bitcast(E4M3X4), scales=aqs[:], in_=ai[:].rearrange("p n t -> p (n t)"))
            st["aq", c] = (aq, aqs)

        def second_matmul(c):
            aq, aqs = st.pop(("aq", c))
            z = psum.tile([P, CHUNKS[c]], F32, name="z", bufs=1)
            nc.tensor.matmul_mx(
                out=z[:],
                lhsT=w2[:].bitcast(E2M1X4),
                lhsT_scale=s_raw[:, HID : HID + CH],
                rhs=aq[:].bitcast(E4M3X4),
                rhs_scale=aqs[:],
                start=True,
                stop=True,
            )
            st["z", c] = z

        def bias_z(c):
            z = st.pop(("z", c))
            zb = work.tile([P, CHUNKS[c]], F32, name="zb")
            nc.scalar.activation(out=zb[:], in_=z[:], func=ACT.Identity, bias=b2f[:])
            st["zb", c] = zb

        def rotate(c):
            zb = st.pop(("zb", c))
            slots = chunk_home[c][2]
            r = psum.tile([P, slots, CH], F32, name="r", bufs=2)
            for j in range(slots):
                nc.tensor.matmul(out=r[:, j, :], lhsT=zb[:, j * P : (j + 1) * P], rhs=rot[:], start=True, stop=True)
            st["r", c] = r

        def norms(c):
            r = st["r", c]
            slots = chunk_home[c][2]
            ss = work.tile([P, slots], F32, name="ss")
            gain = work.tile([P, slots], F32, name="gain")
            for j in range(slots):
                junk = work.tile([P, CH], BF16, name="junk")
                nc.scalar.activation(out=junk[:], in_=r[:, j, :], func=ACT.Square, accum_out=ss[:, j : j + 1])
            nc.scalar.activation(
                out=gain[:], in_=ss[:], func=ACT.Abs_reciprocal_sqrt, scale=inv[:], bias=flag[:]
            )
            st["gain", c] = gain

        def finish(c):
            g, j0, n_slots = chunk_home[c]
            r = st.pop(("r", c))
            gain = st.pop(("gain", c))
            y = work.tile([P, n_slots, CH], F32, name="y")
            for j in range(n_slots):
                nc.vector.scalar_tensor_tensor(
                    out=y[:, j, :],
                    in0=r[:, j, :],
                    scalar=gain[:, j : j + 1],
                    in1=noise_sb[g][:, j0 + j, :],
                    op0=ALU.mult,
                    op1=ALU.add,
                )
            b, size, slots = loads[g][2:]
            dst = out[b : b + size, :].rearrange("(p j) n -> p j n", j=slots)
            nc.sync.dma_start(out=dst[:, j0 : j0 + n_slots, :], in_=y[:])

        n = len(CHUNKS)
        order = [
            (finish, 13),
            (interleave, 8),
            (relu, 5),
            (second_matmul, 9),
            (scale_x, 4),
            (quant_a, 8),
            (rotate, 11),
            (widen, 0),
            (transposes, 3),
            (quant_x, 4),
            (bias_z, 9),
            (first_matmul, 4),
            (widen_v, 0),
            (norms, 11),
        ]
        with tc.manual_schedule():
            for s in range(n + 14):
                if s == 1:
                    weight_scales()
                for stage, lag in order:
                    c = s - lag
                    if 0 <= c < n:
                        stage(c)
